import numpy as np
import ml_dtypes


def mxq(x, axis, fmt="e4m3"):
    dtype, down = {"e4m3": (ml_dtypes.float8_e4m3fn, 7), "e5m2": (ml_dtypes.float8_e5m2, 14)}[fmt]
    v = np.moveaxis(np.asarray(x, np.float32).astype(ml_dtypes.bfloat16).astype(np.float64), axis, -1)
    blocks = v.reshape(v.shape[:-1] + (-1, 32))
    amax = np.abs(blocks).max(-1, keepdims=True)
    byte = np.maximum(np.where(amax > 0, np.frexp(amax)[1] - 1 + 127, 0) - down, 1)
    scale = np.exp2(byte - 127.0)
    codes = (blocks / scale).astype(np.float32).astype(dtype).astype(np.float64)
    return np.moveaxis((codes * scale).reshape(v.shape), -1, axis)


WIDE = False


def mx_kscale(k):
    if not WIDE:
        return np.ones(k)
    levels = np.array([10, -10, 5, -5, 0])
    if k % 512:
        return np.exp2(np.random.permutation(np.resize(levels, k // 32))).repeat(32)
    a = np.empty((k // 512, 16))
    for p in range(k // 512):
        a[p, :8] = np.random.permutation(np.resize(levels, 8))
        for g in range(8):
            far = levels[np.abs(levels - a[p, g]) >= 10]
            a[p, g + 8] = far[np.random.randint(len(far))]
    return np.exp2(a.ravel()).repeat(32)


BF16 = ml_dtypes.bfloat16


def bf(x):
    return np.asarray(x, np.float32).astype(BF16)


def f64(x):
    return np.asarray(x).astype(np.float64)


P, D, B = 8, 512, 128
LAMBDA = 0.1
JJ, II = np.nonzero(1 - np.eye(P, dtype=np.int64))


def setup_inputs():
    s = mx_kscale(D)
    s = s / s.max()
    return {"F": bf(np.random.standard_normal((P, D, B)) * s[:, None]),
            "R": bf(np.random.standard_normal((P, P, D, D)) / np.sqrt(D * (P - 1)) / s)}


def reference(F, R):
    p = F.shape[0]
    Fq = mxq(f64(F), 1, "e4m3")
    Rq = mxq(f64(R)[II, JJ], 2, "e4m3")
    Fi = Fq[II]
    agg = Rq.reshape(P, P - 1, D, D).transpose(0, 2, 1, 3).reshape(P, D, (P - 1) * D) @ Fi.reshape(P, (P - 1) * D, B)
    updated = (f64(F) + agg) / p
    M = np.zeros((P, P, D, B))
    M[II, JJ] = Rq @ Fi
    Dif = M - M.swapaxes(0, 1)
    loss = LAMBDA * 0.5 * np.sum(Dif * Dif)
    return updated, loss

@@ -1,0 +1,268 @@
+from contextlib import ExitStack
+
+import concourse.mybir as mybir
+from concourse.masks import make_identity
+
+F32 = mybir.dt.float32
+BF16 = mybir.dt.bfloat16
+U32 = mybir.dt.uint32
+U8 = mybir.dt.uint8
+FP8X4 = mybir.dt.float8_e4m3fn_x4
+ALU = mybir.AluOpType
+ACT = mybir.ActivationFunctionType
+
+NP = 8
+D = 512
+B = 128
+P = 128
+LOSS_WEIGHT = 0.1 * 0.5 * 2.0
+
+FLOPS = 2 * NP * (NP - 1) * D * D * B
+BYTES = NP * (NP - 1) * D * D * 2 + NP * D * B * 2 + NP * D * B * 4 + 4
+
+MANUAL = True
+RAW_BUFS = 4
+GROUPED_BUFS = 2
+SCALAR_TAKES_ALL = (0, 1, 3, 5)
+
+
+def tile_sheaflayer_kernel(tc, F, R, out_0, out_1):
+    nc = tc.nc
+    units = [(i, j) for i in range(NP) for j in range(i + 1, NP)]
+    n_units = len(units)
+    unit_of = dict((pair, n) for n, pair in enumerate(units))
+    pending = dict((j, []) for j in range(NP))
+    count = dict((j, 0) for j in range(NP))
+    closed_in = {}
+    live = []
+    early = []
+    for n, (i, j) in enumerate(units):
+        pending[j].append(i)
+        pending[i].append(j)
+        live.append([])
+        early.append([])
+        for k in range(NP):
+            if k in closed_in:
+                continue
+            if k == NP - 1:
+                may = n >= n_units - 2
+            else:
+                may = k < 2 or (k - 2 in closed_in and closed_in[k - 2] < n)
+            if not may:
+                continue
+            for i_src in pending[k]:
+                (live if k == i else early)[n].append((k, i_src))
+                count[k] += 1
+            pending[k] = []
+            if count[k] == NP - 1:
+                closed_in[k] = n
+
+    with ExitStack() as ctx:
+        if MANUAL:
+            ctx.enter_context(tc.manual_schedule())
+        keep = ctx.enter_context(tc.tile_pool(name="keep", bufs=1))
+        rawpool = ctx.enter_context(tc.tile_pool(name="rawpool", bufs=RAW_BUFS))
+        gpool = ctx.enter_context(tc.tile_pool(name="gpool", bufs=GROUPED_BUFS))
+        fpool = ctx.enter_context(tc.tile_pool(name="fpool", bufs=2))
+        opool = ctx.enter_context(tc.tile_pool(name="opool", bufs=3))
+        psum = ctx.enter_context(tc.psum_pool(name="psum", bufs=1))
+
+        ident = keep.tile([P, P], F32, name="ident")
+        make_identity(nc, ident[:])
+        zt = keep.tile([P, P], F32, name="zt")
+        nc.vector.memset(zt[:], 0.0)
+        acc = keep.tile([P, n_units], F32, name="acc")
+        tot = keep.tile([P, 1], F32, name="tot")
+        junk = keep.tile([P, D], F32, name="junk")
+        fm = keep.tile([P, NP, D], BF16, name="fm")
+        fcd = [keep.tile([P, B if i == 0 else 2 * B], U32, name="fcd%d" % i, align_bytes=64) for i in range(NP)]
+        fpl = [keep.tile([P, B if i == 0 else 2 * B], U8, name="fpl%d" % i, align_bytes=64) for i in range(NP)]
+        cd = [keep.tile([P, 2 * D], U32, name="cd%d" % n, align_bytes=64) for n in range(n_units)]
+        pl = [keep.tile([P, 2 * D], U8, name="pl%d" % n, align_bytes=64) for n in range(n_units)]
+        raw = {}
+        fg = {}
+        grouped = {}
+        dif = {}
+        agg = {}
+        agg_done = dict((j, 0) for j in range(NP))
+        aggT = {}
+        fin = {}
+
+        def load_f(i):
+            nc.sync.dma_start(out=fm[:, i, :], in_=F[i].rearrange("(q t) b -> q (t b)", t=4))
+
+        def load_unit(n):
+            i, j = units[n]
+            raw[n] = rawpool.tile([P, 8 * D], BF16, name="raw", tag="raw")
+            nc.sync.dma_start(out=raw[n][:, 0 : 4 * D], in_=R[i, j].rearrange("(p c) e -> p (c e)", c=4))
+            nc.sync.dma_start(out=raw[n][:, 4 * D : 8 * D], in_=R[j, i].rearrange("(p c) e -> p (c e)", c=4))
+
+        def regroup_f(i):
+            width = D if i == 0 else 2 * D
+            fg[i] = fpool.tile([P, width], BF16, name="fg", tag="fg", align_bytes=64)
+            nc.vector.tensor_copy(
+                out=fg[i][:, 0:D].rearrange("p (b t) -> p b t", t=4),
+                in_=fm[:, i, :].rearrange("p (t b) -> p b t", t=4),
+            )
+
+        def negate_f(i):
+            if i > 0:
+                nc.vector.tensor_scalar_mul(out=fg[i][:, D : 2 * D], in0=fg[i][:, 0:D], scalar1=-1.0)
+
+        def quantise_f(i):
+            nc.vector.quantize_mx(out=fcd[i][:].bitcast(FP8X4), scales=fpl[i][:], in_=fg[i][:])
+
+        def transpose_unit(n):
+            words = raw[n][:].bitcast(F32)
+            grouped[n] = gpool.tile([P, 8 * D], BF16, name="grouped", tag="grouped", align_bytes=64)
+            g32 = grouped[n][:].bitcast(F32)
+            for b in range(4):
+                tb = psum.tile([P, D], F32, name="tb%d" % b, tag="T%d" % b)
+                for x in range(4):
+                    col = D * b + 2 * P * (x // 2) + x % 2
+                    nc.tensor.transpose(tb[:, P * x : P * (x + 1)], words[:, col : col + 2 * P - 1 : 2], ident[:])
+                src = tb[:].rearrange("p (c u d) -> p c d u", c=2, u=2)
+                dst = g32[:, D * b : D * (b + 1)].rearrange("p (c d u) -> p c d u", c=2, u=2)
+                if b < 3 or n in SCALAR_TAKES_ALL:
+                    nc.scalar.copy(out=dst, in_=src)
+                else:
+                    nc.vector.tensor_copy(out=dst, in_=src)
+
+        def quantise_block(n, s):
+            nc.vector.quantize_mx(
+                out=cd[n][:, D * s : D * (s + 1)].bitcast(FP8X4),
+                scales=pl[n][:, D * s : D * (s + 1)],
+                in_=grouped[n][:, 4 * D * s : 4 * D * (s + 1)],
+            )
+
+        def mx_pass(bank, i_src, sign, n, s, start, stop):
+            nc.tensor.matmul_mx(
+                out=bank[:],
+                lhsT=fcd[i_src][:, B * sign : B * (sign + 1)].bitcast(FP8X4),
+                lhsT_scale=fpl[i_src][:, B * sign : B * (sign + 1)],
+                rhs=cd[n][:, D * s : D * (s + 1)].bitcast(FP8X4),
+                rhs_scale=pl[n][:, D * s : D * (s + 1)],
+                start=start,
+                stop=stop,
+            )
+
+        def agg_passes(todo):
+            for (dst, i_src) in todo:
+                if agg_done[dst] == 0:
+                    tag = "T0" if dst == NP - 1 else "A%d" % (dst % 2)
+                    agg[dst] = psum.tile([P, D], F32, name="agg%d" % dst, tag=tag)
+                if i_src < dst:
+                    where, s = unit_of[(i_src, dst)], 0
+                else:
+                    where, s = unit_of[(dst, i_src)], 1
+                mx_pass(agg[dst], i_src, 0, where, s, agg_done[dst] == 0, agg_done[dst] == NP - 2)
+                agg_done[dst] += 1
+
+        def multiply_unit(n):
+            i, j = units[n]
+            closes = [k for k in range(NP) if closed_in[k] == n]
+            if closes:
+                agg_passes(live[n])
+                if n == n_units - 1:
+                    agg_passes(early[n])
+            dif[n] = psum.tile([P, D], F32, name="dif", tag="D")
+            mx_pass(dif[n], i, 0, n, 0, True, False)
+            mx_pass(dif[n], j, 1, n, 1, False, True)
+            if not closes:
+                agg_passes(live[n])
+            if n < n_units - 1:
+                agg_passes(early[n])
+            return closes
+
+        def square_unit(n):
+            nc.scalar.activation(out=junk[:], in_=dif[n][:], func=ACT.Square, accum_out=acc[:, n : n + 1])
+
+        def evacuate(j, on_scalar):
+            aggT[j] = opool.tile([P, D], F32, name="aggT", tag="aggT")
+            if on_scalar:
+                nc.scalar.mul(out=aggT[j][:], in_=agg[j][:], mul=0.125)
+            else:
+                nc.vector.tensor_scalar_mul(out=aggT[j][:], in0=agg[j][:], scalar1=0.125)
+
+        def transpose_back(j):
+            tag = "X" if j < NP - 2 else "T%d" % (j - NP + 3)
+            fin[j] = psum.tile([P, D], F32, name="fin%d" % j, tag=tag)
+            for t in range(4):
+                nc.tensor.transpose(fin[j][:, P * t : P * (t + 1)], aggT[j][:, P * t : P * (t + 1)], ident[:])
+
+        def finish(j):
+            res = opool.tile([P, D], F32, name="res", tag="res")
+            nc.vector.scalar_tensor_tensor(
+                out=res[:], in0=fm[:, j, :], scalar=0.125, in1=fin[j][:], op0=ALU.mult, op1=ALU.add
+            )
+            nc.sync.dma_start(out=out_0[j].rearrange("(q t) b -> q (t b)", t=4), in_=res[:])
+
+        load_unit(0)
+        load_f(0)
+        load_f(1)
+        load_f(2)
+        for n in range(1, RAW_BUFS):
+            load_unit(n)
+            if n + 2 < NP:
+                load_f(n + 2)
+
+        waiting = []
+        for n in range(n_units - 1):
+            transpose_unit(n)
+            back = waiting
+            for j in back:
+                transpose_back(j)
+            waiting = []
+            if n >= 2:
+                waiting = multiply_unit(n - 2)
+                square_unit(n - 2)
+                for j in waiting:
+                    evacuate(j, False)
+            new_f = [i for i in range(NP) if (i == 0 and n == 0) or i == n + 1]
+            for i in new_f:
+                regroup_f(i)
+            quantise_block(n, 0)
+            for i in new_f:
+                negate_f(i)
+            quantise_block(n, 1)
+            for i in new_f:
+                quantise_f(i)
+            for j in back:
+                finish(j)
+            if n + RAW_BUFS < n_units:
+                load_unit(n + RAW_BUFS)
+                if n + RAW_BUFS + 2 < NP:
+                    load_f(n + RAW_BUFS + 2)
+
+        n = n_units - 1
+        transpose_unit(n)
+        for j in waiting:
+            transpose_back(j)
+        quantise_block(n, 0)
+        quantise_block(n, 1)
+        for j in waiting:
+            finish(j)
+        multiply_unit(n - 2)
+        square_unit(n - 2)
+        multiply_unit(n - 1)
+        square_unit(n - 1)
+        evacuate(NP - 3, False)
+        transpose_back(NP - 3)
+        finish(NP - 3)
+        multiply_unit(n)
+        evacuate(NP - 2, False)
+        evacuate(NP - 1, True)
+        square_unit(n)
+        transpose_back(NP - 2)
+        transpose_back(NP - 1)
+        finish(NP - 2)
+        nc.vector.reduce_sum(out=zt[:, 0:1], in_=acc[:], axis=mybir.AxisListType.X)
+        finish(NP - 1)
+
+        lt = psum.tile([P, D], F32, name="lt", tag="T3")
+        nc.tensor.transpose(lt[:, 0:P], zt[:], ident[:])
+        nc.scalar.activation(out=junk[:, 0:P], in_=lt[:, 0:P], func=ACT.Copy, scale=LOSS_WEIGHT, accum_out=tot[:, 0:1])
+        loss_view = out_1
+        for k in range(2 - len(out_1.shape)):
+            loss_view = loss_view.unsqueeze(0)
+        nc.sync.dma_start(out=loss_view, in_=tot[0:1, 0:1])

@@ -20,10 +20,10 @@ LOSS_WEIGHT = 0.1 * 0.5 * 2.0
 FLOPS = 2 * NP * (NP - 1) * D * D * B
 BYTES = NP * (NP - 1) * D * D * 2 + NP * D * B * 2 + NP * D * B * 4 + 4
 
-MANUAL = True
-RAW_BUFS = 4
-GROUPED_BUFS = 2
-SCALAR_TAKES_ALL = (0, 1, 3, 5)
+RAW_BUFS = 6
+SPLIT_BUFS = 3
+GROUPED_BUFS = 4
+AHEAD = 4
 
 
 def tile_sheaflayer_kernel(tc, F, R, out_0, out_1):
@@ -58,13 +58,13 @@ def tile_sheaflayer_kernel(tc, F, R, out_0, out_1):
                 closed_in[k] = n
 
     with ExitStack() as ctx:
-        if MANUAL:
-            ctx.enter_context(tc.manual_schedule())
+        ctx.enter_context(tc.manual_schedule())
         keep = ctx.enter_context(tc.tile_pool(name="keep", bufs=1))
         rawpool = ctx.enter_context(tc.tile_pool(name="rawpool", bufs=RAW_BUFS))
+        spool = ctx.enter_context(tc.tile_pool(name="spool", bufs=SPLIT_BUFS))
         gpool = ctx.enter_context(tc.tile_pool(name="gpool", bufs=GROUPED_BUFS))
         fpool = ctx.enter_context(tc.tile_pool(name="fpool", bufs=2))
-        opool = ctx.enter_context(tc.tile_pool(name="opool", bufs=3))
+        opool = ctx.enter_context(tc.tile_pool(name="opool", bufs=2))
         psum = ctx.enter_context(tc.psum_pool(name="psum", bufs=1))
 
         ident = keep.tile([P, P], F32, name="ident")
@@ -81,6 +81,7 @@ def tile_sheaflayer_kernel(tc, F, R, out_0, out_1):
         pl = [keep.tile([P, 2 * D], U8, name="pl%d" % n, align_bytes=64) for n in range(n_units)]
         raw = {}
         fg = {}
+        split = {}
         grouped = {}
         dif = {}
         agg = {}
@@ -93,9 +94,16 @@ def tile_sheaflayer_kernel(tc, F, R, out_0, out_1):
 
         def load_unit(n):
             i, j = units[n]
-            raw[n] = rawpool.tile([P, 8 * D], BF16, name="raw", tag="raw")
-            nc.sync.dma_start(out=raw[n][:, 0 : 4 * D], in_=R[i, j].rearrange("(p c) e -> p (c e)", c=4))
-            nc.sync.dma_start(out=raw[n][:, 4 * D : 8 * D], in_=R[j, i].rearrange("(p c) e -> p (c e)", c=4))
+            for s, block in ((0, R[i, j]), (1, R[j, i])):
+                raw[n, s] = rawpool.tile([P, 4 * D], BF16, name="raw", tag="raw")
+                nc.sync.dma_start(out=raw[n, s][:], in_=block.rearrange("(p c) e -> p (c e)", c=4))
+
+        def split_block(n, s):
+            split[n, s] = spool.tile([P, 2 * D], F32, name="split", tag="split")
+            nc.vector.tensor_copy(
+                out=split[n, s][:].rearrange("p (c u q) -> p c u q", c=4, u=2),
+                in_=raw[n, s][:].bitcast(F32).rearrange("p (c q u) -> p c u q", c=4, u=2),
+            )
 
         def regroup_f(i):
             width = D if i == 0 else 2 * D
@@ -113,26 +121,31 @@ def tile_sheaflayer_kernel(tc, F, R, out_0, out_1):
             nc.vector.quantize_mx(out=fcd[i][:].bitcast(FP8X4), scales=fpl[i][:], in_=fg[i][:])
 
         def transpose_unit(n):
-            words = raw[n][:].bitcast(F32)
-            grouped[n] = gpool.tile([P, 8 * D], BF16, name="grouped", tag="grouped", align_bytes=64)
-            g32 = grouped[n][:].bitcast(F32)
             for b in range(4):
+                s = b // 2
+                if b % 2 == 0:
+                    grouped[n, s] = gpool.tile([P, 4 * D], BF16, name="grouped", tag="grouped", align_bytes=64)
                 tb = psum.tile([P, D], F32, name="tb%d" % b, tag="T%d" % b)
                 for x in range(4):
-                    col = D * b + 2 * P * (x // 2) + x % 2
-                    nc.tensor.transpose(tb[:, P * x : P * (x + 1)], words[:, col : col + 2 * P - 1 : 2], ident[:])
-                src = tb[:].rearrange("p (c u d) -> p c d u", c=2, u=2)
-                dst = g32[:, D * b : D * (b + 1)].rearrange("p (c d u) -> p c d u", c=2, u=2)
-                if b < 3 or n in SCALAR_TAKES_ALL:
-                    nc.scalar.copy(out=dst, in_=src)
-                else:
-                    nc.vector.tensor_copy(out=dst, in_=src)
+                    if n == 0:
+                        col = D * (b % 2) + 2 * P * (x // 2) + x % 2
+                        src = raw[n, s][:].bitcast(F32)[:, col : col + 2 * P - 1 : 2]
+                    else:
+                        col = D * (b % 2) + P * x
+                        src = split[n, s][:, col : col + P]
+                    nc.tensor.transpose(tb[:, P * x : P * (x + 1)], src, ident[:])
+                nc.scalar.copy(
+                    out=grouped[n, s][:]
+                    .bitcast(F32)[:, D * (b % 2) : D * (b % 2 + 1)]
+                    .rearrange("p (c d u) -> p c d u", c=2, u=2),
+                    in_=tb[:].rearrange("p (c u d) -> p c d u", c=2, u=2),
+                )
 
         def quantise_block(n, s):
             nc.vector.quantize_mx(
                 out=cd[n][:, D * s : D * (s + 1)].bitcast(FP8X4),
                 scales=pl[n][:, D * s : D * (s + 1)],
-                in_=grouped[n][:, 4 * D * s : 4 * D * (s + 1)],
+                in_=grouped[n, s][:],
             )
 
         def mx_pass(bank, i_src, sign, n, s, start, stop):
@@ -201,10 +214,9 @@ def tile_sheaflayer_kernel(tc, F, R, out_0, out_1):
         load_f(0)
         load_f(1)
         load_f(2)
-        for n in range(1, RAW_BUFS):
+        for n in range(1, AHEAD):
             load_unit(n)
-            if n + 2 < NP:
-                load_f(n + 2)
+            load_f(n + 2)
 
         waiting = []
         for n in range(n_units - 1):
@@ -221,18 +233,25 @@ def tile_sheaflayer_kernel(tc, F, R, out_0, out_1):
             new_f = [i for i in range(NP) if (i == 0 and n == 0) or i == n + 1]
             for i in new_f:
                 regroup_f(i)
+            if n == 0:
+                split_block(1, 0)
+                split_block(1, 1)
             quantise_block(n, 0)
             for i in new_f:
                 negate_f(i)
+            if n + 2 < n_units:
+                split_block(n + 2, 0)
             quantise_block(n, 1)
             for i in new_f:
                 quantise_f(i)
+            if n + 2 < n_units:
+                split_block(n + 2, 1)
             for j in back:
                 finish(j)
-            if n + RAW_BUFS < n_units:
-                load_unit(n + RAW_BUFS)
-                if n + RAW_BUFS + 2 < NP:
-                    load_f(n + RAW_BUFS + 2)
+            if n + AHEAD < n_units:
+                load_unit(n + AHEAD)
+                if n + AHEAD + 2 < NP:
+                    load_f(n + AHEAD + 2)
 
         n = n_units - 1
         transpose_unit(n)

@@ -20,42 +20,24 @@ LOSS_WEIGHT = 0.1 * 0.5 * 2.0
 FLOPS = 2 * NP * (NP - 1) * D * D * B
 BYTES = NP * (NP - 1) * D * D * 2 + NP * D * B * 2 + NP * D * B * 4 + 4
 
-RAW_BUFS = 6
-SPLIT_BUFS = 3
-GROUPED_BUFS = 4
-AHEAD = 4
+RAW_BUFS = 8
+SPLIT_BUFS = 4
+GROUPED_BUFS = 3
+STRIDED = ((0, 0), (0, 1), (1, 1), (2, 1), (3, 1), (4, 1), (5, 1), (6, 1))
+VECTOR_BANKS = ()
+LAG = 2
+MAX_AGG = 3
 
 
 def tile_sheaflayer_kernel(tc, F, R, out_0, out_1):
     nc = tc.nc
     units = [(i, j) for i in range(NP) for j in range(i + 1, NP)]
     n_units = len(units)
+    last = n_units - 1
     unit_of = dict((pair, n) for n, pair in enumerate(units))
-    pending = dict((j, []) for j in range(NP))
-    count = dict((j, 0) for j in range(NP))
-    closed_in = {}
-    live = []
-    early = []
-    for n, (i, j) in enumerate(units):
-        pending[j].append(i)
-        pending[i].append(j)
-        live.append([])
-        early.append([])
-        for k in range(NP):
-            if k in closed_in:
-                continue
-            if k == NP - 1:
-                may = n >= n_units - 2
-            else:
-                may = k < 2 or (k - 2 in closed_in and closed_in[k - 2] < n)
-            if not may:
-                continue
-            for i_src in pending[k]:
-                (live if k == i else early)[n].append((k, i_src))
-                count[k] += 1
-            pending[k] = []
-            if count[k] == NP - 1:
-                closed_in[k] = n
+
+    def where(i, j):
+        return (unit_of[(i, j)], 0) if i < j else (unit_of[(j, i)], 1)
 
     with ExitStack() as ctx:
         ctx.enter_context(tc.manual_schedule())
@@ -64,13 +46,13 @@ def tile_sheaflayer_kernel(tc, F, R, out_0, out_1):
         spool = ctx.enter_context(tc.tile_pool(name="spool", bufs=SPLIT_BUFS))
         gpool = ctx.enter_context(tc.tile_pool(name="gpool", bufs=GROUPED_BUFS))
         fpool = ctx.enter_context(tc.tile_pool(name="fpool", bufs=2))
-        opool = ctx.enter_context(tc.tile_pool(name="opool", bufs=2))
+        opool = ctx.enter_context(tc.tile_pool(name="opool", bufs=3))
         psum = ctx.enter_context(tc.psum_pool(name="psum", bufs=1))
 
         ident = keep.tile([P, P], F32, name="ident")
         make_identity(nc, ident[:])
-        zt = keep.tile([P, P], F32, name="zt")
-        nc.vector.memset(zt[:], 0.0)
+        ones = keep.tile([P, P], F32, name="ones")
+        nc.vector.memset(ones[:], 1.0)
         acc = keep.tile([P, n_units], F32, name="acc")
         tot = keep.tile([P, 1], F32, name="tot")
         junk = keep.tile([P, D], F32, name="junk")
@@ -92,22 +74,22 @@ def tile_sheaflayer_kernel(tc, F, R, out_0, out_1):
         def load_f(i):
             nc.sync.dma_start(out=fm[:, i, :], in_=F[i].rearrange("(q t) b -> q (t b)", t=4))
 
-        def load_unit(n):
-            i, j = units[n]
-            for s, block in ((0, R[i, j]), (1, R[j, i])):
-                raw[n, s] = rawpool.tile([P, 4 * D], BF16, name="raw", tag="raw")
-                nc.sync.dma_start(out=raw[n, s][:], in_=block.rearrange("(p c) e -> p (c e)", c=4))
+        def load_block(n, s):
+            i, j = units[n] if s == 0 else units[n][::-1]
+            raw[n, s] = rawpool.tile([P, 4 * D], BF16, name="raw", tag="raw")
+            nc.sync.dma_start(out=raw[n, s][:], in_=R[i, j].rearrange("(p c) e -> p (c e)", c=4))
 
         def split_block(n, s):
-            split[n, s] = spool.tile([P, 2 * D], F32, name="split", tag="split")
-            nc.vector.tensor_copy(
-                out=split[n, s][:].rearrange("p (c u q) -> p c u q", c=4, u=2),
-                in_=raw[n, s][:].bitcast(F32).rearrange("p (c q u) -> p c u q", c=4, u=2),
-            )
+            if (n, s) not in STRIDED:
+                consumed.add((n, s))
+                split[n, s] = spool.tile([P, 2 * D], F32, name="split", tag="split")
+                nc.vector.tensor_copy(
+                    out=split[n, s][:].rearrange("p (c u q) -> p c u q", c=4, u=2),
+                    in_=raw[n, s][:].bitcast(F32).rearrange("p (c q u) -> p c u q", c=4, u=2),
+                )
 
         def regroup_f(i):
-            width = D if i == 0 else 2 * D
-            fg[i] = fpool.tile([P, width], BF16, name="fg", tag="fg", align_bytes=64)
+            fg[i] = fpool.tile([P, D if i == 0 else 2 * D], BF16, name="fg", tag="fg", align_bytes=64)
             nc.vector.tensor_copy(
                 out=fg[i][:, 0:D].rearrange("p (b t) -> p b t", t=4),
                 in_=fm[:, i, :].rearrange("p (t b) -> p b t", t=4),
@@ -127,19 +109,24 @@ def tile_sheaflayer_kernel(tc, F, R, out_0, out_1):
                     grouped[n, s] = gpool.tile([P, 4 * D], BF16, name="grouped", tag="grouped", align_bytes=64)
                 tb = psum.tile([P, D], F32, name="tb%d" % b, tag="T%d" % b)
                 for x in range(4):
-                    if n == 0:
+                    if (n, s) in STRIDED:
+                        consumed.add((n, s))
                         col = D * (b % 2) + 2 * P * (x // 2) + x % 2
                         src = raw[n, s][:].bitcast(F32)[:, col : col + 2 * P - 1 : 2]
                     else:
                         col = D * (b % 2) + P * x
                         src = split[n, s][:, col : col + P]
                     nc.tensor.transpose(tb[:, P * x : P * (x + 1)], src, ident[:])
-                nc.scalar.copy(
-                    out=grouped[n, s][:]
+                dst = (
+                    grouped[n, s][:]
                     .bitcast(F32)[:, D * (b % 2) : D * (b % 2 + 1)]
-                    .rearrange("p (c d u) -> p c d u", c=2, u=2),
-                    in_=tb[:].rearrange("p (c u d) -> p c d u", c=2, u=2),
+                    .rearrange("p (c d u) -> p c d u", c=2, u=2)
                 )
+                src = tb[:].rearrange("p (c u d) -> p c d u", c=2, u=2)
+                if (n, b) in VECTOR_BANKS:
+                    nc.vector.tensor_copy(out=dst, in_=src)
+                else:
+                    nc.scalar.copy(out=dst, in_=src)
 
         def quantise_block(n, s):
             nc.vector.quantize_mx(
@@ -148,7 +135,7 @@ def tile_sheaflayer_kernel(tc, F, R, out_0, out_1):
                 in_=grouped[n, s][:],
             )
 
-        def mx_pass(bank, i_src, sign, n, s, start, stop):
+        def row_pass(bank, i_src, sign, n, s, start, stop):
             nc.tensor.matmul_mx(
                 out=bank[:],
                 lhsT=fcd[i_src][:, B * sign : B * (sign + 1)].bitcast(FP8X4),
@@ -159,46 +146,30 @@ def tile_sheaflayer_kernel(tc, F, R, out_0, out_1):
                 stop=stop,
             )
 
-        def agg_passes(todo):
-            for (dst, i_src) in todo:
-                if agg_done[dst] == 0:
-                    tag = "T0" if dst == NP - 1 else "A%d" % (dst % 2)
-                    agg[dst] = psum.tile([P, D], F32, name="agg%d" % dst, tag=tag)
-                if i_src < dst:
-                    where, s = unit_of[(i_src, dst)], 0
-                else:
-                    where, s = unit_of[(dst, i_src)], 1
-                mx_pass(agg[dst], i_src, 0, where, s, agg_done[dst] == 0, agg_done[dst] == NP - 2)
-                agg_done[dst] += 1
-
-        def multiply_unit(n):
+        def dif_passes(n):
             i, j = units[n]
-            closes = [k for k in range(NP) if closed_in[k] == n]
-            if closes:
-                agg_passes(live[n])
-                if n == n_units - 1:
-                    agg_passes(early[n])
             dif[n] = psum.tile([P, D], F32, name="dif", tag="D")
-            mx_pass(dif[n], i, 0, n, 0, True, False)
-            mx_pass(dif[n], j, 1, n, 1, False, True)
-            if not closes:
-                agg_passes(live[n])
-            if n < n_units - 1:
-                agg_passes(early[n])
-            return closes
+            row_pass(dif[n], i, 0, n, 0, True, False)
+            row_pass(dif[n], j, 1, n, 1, False, True)
+
+        def agg_pass(j, i):
+            if agg_done[j] == 0:
+                agg[j] = psum.tile([P, D], F32, name="agg%d" % j, tag="A%d" % (j % 3))
+            n, s = where(i, j)
+            row_pass(agg[j], i, 0, n, s, agg_done[j] == 0, agg_done[j] == NP - 2)
+            agg_done[j] += 1
 
         def square_unit(n):
             nc.scalar.activation(out=junk[:], in_=dif[n][:], func=ACT.Square, accum_out=acc[:, n : n + 1])
 
         def evacuate(j, on_scalar):
-            aggT[j] = opool.tile([P, D], F32, name="aggT", tag="aggT")
+            aggT[j] = opool.tile([P, D], F32, name="aggT", tag="aggT", bufs=2)
             if on_scalar:
                 nc.scalar.mul(out=aggT[j][:], in_=agg[j][:], mul=0.125)
             else:
                 nc.vector.tensor_scalar_mul(out=aggT[j][:], in0=agg[j][:], scalar1=0.125)
 
-        def transpose_back(j):
-            tag = "X" if j < NP - 2 else "T%d" % (j - NP + 3)
+        def transpose_back(j, tag):
             fin[j] = psum.tile([P, D], F32, name="fin%d" % j, tag=tag)
             for t in range(4):
                 nc.tensor.transpose(fin[j][:, P * t : P * (t + 1)], aggT[j][:, P * t : P * (t + 1)], ident[:])
@@ -210,77 +181,108 @@ def tile_sheaflayer_kernel(tc, F, R, out_0, out_1):
             )
             nc.sync.dma_start(out=out_0[j].rearrange("(q t) b -> q (t b)", t=4), in_=res[:])
 
-        load_unit(0)
-        load_f(0)
-        load_f(1)
-        load_f(2)
-        for n in range(1, AHEAD):
-            load_unit(n)
-            load_f(n + 2)
+        blocks = [(n, s) for n in range(n_units) for s in range(2)]
 
-        waiting = []
-        for n in range(n_units - 1):
+        consumed = set()
+
+        def load_more():
+            k = len(raw)
+            while k < len(blocks) and (k < RAW_BUFS or blocks[k - RAW_BUFS] in consumed):
+                load_block(*blocks[k])
+                k += 1
+
+        for k in range(RAW_BUFS):
+            load_block(*blocks[k])
+            if k == 1:
+                load_f(0)
+                load_f(1)
+            elif k % 2 == 1:
+                load_f(k // 2 + 1)
+
+        pending = dict((j, []) for j in range(NP))
+        free = set(range(3))
+        closed = []
+        to_back = []
+        to_finish = []
+        freed = []
+
+        def multiply_unit(n, most):
+            i, j = units[n]
+            pending[j].append(i)
+            pending[i].append(j)
+            todo = [(k, src) for k in range(NP) if k in free for src in pending[k] if (k, src) not in ((i, j), (j, i))]
+            todo += [(j, i)] if j in free else []
+            todo += [(i, j)] if i in free else []
+            for k, src in todo[0:most]:
+                pending[k].remove(src)
+                agg_pass(k, src)
+                if agg_done[k] == NP - 1:
+                    closed.append(k)
+            dif_passes(n)
+
+        for n in range(n_units):
             transpose_unit(n)
-            back = waiting
-            for j in back:
-                transpose_back(j)
-            waiting = []
-            if n >= 2:
-                waiting = multiply_unit(n - 2)
-                square_unit(n - 2)
-                for j in waiting:
-                    evacuate(j, False)
-            new_f = [i for i in range(NP) if (i == 0 and n == 0) or i == n + 1]
-            for i in new_f:
-                regroup_f(i)
+            leaving = closed
+            closed = []
+            ending = to_finish
+            to_finish = to_back
+            to_back = []
+            for j in freed:
+                free.add(j + 3)
+            freed = ending
+            if n >= LAG:
+                multiply_unit(n - LAG, MAX_AGG)
+                square_unit(n - LAG)
+            for j in leaving:
+                evacuate(j, False)
+                to_back.append(j)
+            for j in to_back:
+                transpose_back(j, "A%d" % (j % 3))
+            for j in ending:
+                finish(j)
             if n == 0:
+                regroup_f(0)
+                regroup_f(1)
                 split_block(1, 0)
                 split_block(1, 1)
-            quantise_block(n, 0)
-            for i in new_f:
-                negate_f(i)
-            if n + 2 < n_units:
-                split_block(n + 2, 0)
-            quantise_block(n, 1)
-            for i in new_f:
-                quantise_f(i)
-            if n + 2 < n_units:
-                split_block(n + 2, 1)
-            for j in back:
-                finish(j)
-            if n + AHEAD < n_units:
-                load_unit(n + AHEAD)
-                if n + AHEAD + 2 < NP:
-                    load_f(n + AHEAD + 2)
+            elif n + 1 < NP:
+                regroup_f(n + 1)
+            new_f = [i for i in range(NP) if (i == 0 and n == 0) or i == n + 1]
+            for s in range(2):
+                quantise_block(n, s)
+                if s == 0:
+                    for i in new_f:
+                        negate_f(i)
+                else:
+                    for i in new_f:
+                        quantise_f(i)
+                if n + 2 < n_units:
+                    split_block(n + 2, s)
+                load_more()
+            if n + 5 < NP:
+                load_f(n + 5)
 
-        n = n_units - 1
-        transpose_unit(n)
-        for j in waiting:
-            transpose_back(j)
-        quantise_block(n, 0)
-        quantise_block(n, 1)
-        for j in waiting:
+        for j in to_finish + to_back:
             finish(j)
-        multiply_unit(n - 2)
-        square_unit(n - 2)
-        multiply_unit(n - 1)
-        square_unit(n - 1)
-        evacuate(NP - 3, False)
-        transpose_back(NP - 3)
-        finish(NP - 3)
-        multiply_unit(n)
-        evacuate(NP - 2, False)
-        evacuate(NP - 1, True)
-        square_unit(n)
-        transpose_back(NP - 2)
-        transpose_back(NP - 1)
-        finish(NP - 2)
-        nc.vector.reduce_sum(out=zt[:, 0:1], in_=acc[:], axis=mybir.AxisListType.X)
-        finish(NP - 1)
+        for j in freed + to_finish + to_back:
+            free.add(j + 3)
+        tail = []
+        for n in range(n_units - LAG, n_units):
+            multiply_unit(n, NP * NP)
+            for j in closed:
+                evacuate(j, j != 6)
+                tail.append(j)
+            closed = []
+            square_unit(n)
+        for j in tail:
+            transpose_back(j, "T%d" % (j - 4))
+            finish(j)
 
-        lt = psum.tile([P, D], F32, name="lt", tag="T3")
-        nc.tensor.transpose(lt[:, 0:P], zt[:], ident[:])
-        nc.scalar.activation(out=junk[:, 0:P], in_=lt[:, 0:P], func=ACT.Copy, scale=LOSS_WEIGHT, accum_out=tot[:, 0:1])
+        lt = psum.tile([P, n_units], F32, name="lt", tag="T0")
+        nc.tensor.matmul(lt[:], lhsT=ones[:], rhs=acc[:], start=True, stop=True)
+        nc.scalar.activation(
+            out=junk[:, 0:n_units], in_=lt[:], func=ACT.Copy, scale=LOSS_WEIGHT, accum_out=tot[:, 0:1]
+        )
         loss_view = out_1
         for k in range(2 - len(out_1.shape)):
             loss_view = loss_view.unsqueeze(0)

@@ -84,8 +84,8 @@ def tile_sheaflayer_kernel(tc, F, R, out_0, out_1):
                 consumed.add((n, s))
                 split[n, s] = spool.tile([P, 2 * D], F32, name="split", tag="split")
                 nc.vector.tensor_copy(
-                    out=split[n, s][:].rearrange("p (c u q) -> p c u q", c=4, u=2),
-                    in_=raw[n, s][:].bitcast(F32).rearrange("p (c q u) -> p c u q", c=4, u=2),
+                    out=split[n, s][:].rearrange("p (c u q) -> p c q u", c=4, u=2),
+                    in_=raw[n, s][:].bitcast(F32).rearrange("p (c q u) -> p c q u", c=4, u=2),
                 )
 
         def regroup_f(i):

@@ -22,7 +22,7 @@ BYTES = NP * (NP - 1) * D * D * 2 + NP * D * B * 2 + NP * D * B * 4 + 4
 
 RAW_BUFS = 8
 SPLIT_BUFS = 4
-GROUPED_BUFS = 3
+GROUPED_BUFS = 4
 STRIDED = ((0, 0), (0, 1), (1, 1), (2, 1), (3, 1), (4, 1), (5, 1), (6, 1))
 VECTOR_BANKS = ()
 LAG = 2
@@ -163,7 +163,7 @@ def tile_sheaflayer_kernel(tc, F, R, out_0, out_1):
             nc.scalar.activation(out=junk[:], in_=dif[n][:], func=ACT.Square, accum_out=acc[:, n : n + 1])
 
         def evacuate(j, on_scalar):
-            aggT[j] = opool.tile([P, D], F32, name="aggT", tag="aggT", bufs=2)
+            aggT[j] = opool.tile([P, D], F32, name="aggT", tag="aggT")
             if on_scalar:
                 nc.scalar.mul(out=aggT[j][:], in_=agg[j][:], mul=0.125)
             else:
@@ -175,7 +175,7 @@ def tile_sheaflayer_kernel(tc, F, R, out_0, out_1):
                 nc.tensor.transpose(fin[j][:, P * t : P * (t + 1)], aggT[j][:, P * t : P * (t + 1)], ident[:])
 
         def finish(j):
-            res = opool.tile([P, D], F32, name="res", tag="res")
+            res = aggT[j]
             nc.vector.scalar_tensor_tensor(
                 out=res[:], in0=fm[:, j, :], scalar=0.125, in1=fin[j][:], op0=ALU.mult, op1=ALU.add
             )

@@ -23,10 +23,10 @@ BYTES = NP * (NP - 1) * D * D * 2 + NP * D * B * 2 + NP * D * B * 4 + 4
 RAW_BUFS = 8
 SPLIT_BUFS = 4
 GROUPED_BUFS = 4
-STRIDED = ((0, 0), (0, 1), (1, 1), (2, 1), (3, 1), (4, 1), (5, 1), (6, 1))
-VECTOR_BANKS = ()
+STRIDED = [(n, s) for n in range(9) for s in range(2) if n < 4 or s == 1]
+VECTOR_BANKS = ((26, 1), (27, 1), (27, 3))
 LAG = 2
-MAX_AGG = 3
+N_BURST = 6
 
 
 def tile_sheaflayer_kernel(tc, F, R, out_0, out_1):
@@ -96,6 +96,7 @@ def tile_sheaflayer_kernel(tc, F, R, out_0, out_1):
             )
 
         def negate_f(i):
+            nc.vector.tensor_scalar_mul(out=fm[:, i, :], in0=fm[:, i, :], scalar1=0.125)
             if i > 0:
                 nc.vector.tensor_scalar_mul(out=fg[i][:, D : 2 * D], in0=fg[i][:, 0:D], scalar1=-1.0)
 
@@ -154,20 +155,37 @@ def tile_sheaflayer_kernel(tc, F, R, out_0, out_1):
 
         def agg_pass(j, i):
             if agg_done[j] == 0:
-                agg[j] = psum.tile([P, D], F32, name="agg%d" % j, tag="A%d" % (j % 3))
+                agg[j] = psum.tile([P, D], F32, name="agg%d" % j, tag="A%d" % j)
             n, s = where(i, j)
             row_pass(agg[j], i, 0, n, s, agg_done[j] == 0, agg_done[j] == NP - 2)
             agg_done[j] += 1
+
+        def burst_quarter(j, c, tag):
+            if c == 0:
+                fin[j] = psum.tile([P, D], F32, name="fin%d" % j, tag=tag)
+            sources = [i for i in range(NP) if i != j]
+            for i in sources:
+                n, s = where(i, j)
+                at = D * s + P * c
+                nc.tensor.matmul_mx(
+                    out=fin[j][:, B * c : B * (c + 1)],
+                    lhsT=cd[n][:, at : at + P].bitcast(FP8X4),
+                    lhsT_scale=pl[n][:, at : at + P],
+                    rhs=fcd[i][:, 0:B].bitcast(FP8X4),
+                    rhs_scale=fpl[i][:, 0:B],
+                    start=i == sources[0],
+                    stop=i == sources[-1],
+                )
 
         def square_unit(n):
             nc.scalar.activation(out=junk[:], in_=dif[n][:], func=ACT.Square, accum_out=acc[:, n : n + 1])
 
         def evacuate(j, on_scalar):
-            aggT[j] = opool.tile([P, D], F32, name="aggT", tag="aggT")
+            aggT[j] = spool.tile([P, 2 * D], F32, name="split", tag="split")[:, 0:D]
             if on_scalar:
-                nc.scalar.mul(out=aggT[j][:], in_=agg[j][:], mul=0.125)
+                nc.scalar.copy(out=aggT[j][:], in_=agg[j][:])
             else:
-                nc.vector.tensor_scalar_mul(out=aggT[j][:], in0=agg[j][:], scalar1=0.125)
+                nc.vector.tensor_copy(out=aggT[j][:], in_=agg[j][:])
 
         def transpose_back(j, tag):
             fin[j] = psum.tile([P, D], F32, name="fin%d" % j, tag=tag)
@@ -175,9 +193,9 @@ def tile_sheaflayer_kernel(tc, F, R, out_0, out_1):
                 nc.tensor.transpose(fin[j][:, P * t : P * (t + 1)], aggT[j][:, P * t : P * (t + 1)], ident[:])
 
         def finish(j):
-            res = aggT[j]
+            res = aggT[j] if j in aggT else opool.tile([P, D], F32, name="res", tag="res")
             nc.vector.scalar_tensor_tensor(
-                out=res[:], in0=fm[:, j, :], scalar=0.125, in1=fin[j][:], op0=ALU.mult, op1=ALU.add
+                out=res[:], in0=fin[j][:], scalar=0.125, in1=fm[:, j, :], op0=ALU.mult, op1=ALU.add
             )
             nc.sync.dma_start(out=out_0[j].rearrange("(q t) b -> q (t b)", t=4), in_=res[:])
 
@@ -199,45 +217,33 @@ def tile_sheaflayer_kernel(tc, F, R, out_0, out_1):
             elif k % 2 == 1:
                 load_f(k // 2 + 1)
 
-        pending = dict((j, []) for j in range(NP))
-        free = set(range(3))
-        closed = []
-        to_back = []
+        quarters = []
         to_finish = []
-        freed = []
 
-        def multiply_unit(n, most):
+        def multiply_unit(n):
             i, j = units[n]
-            pending[j].append(i)
-            pending[i].append(j)
-            todo = [(k, src) for k in range(NP) if k in free for src in pending[k] if (k, src) not in ((i, j), (j, i))]
-            todo += [(j, i)] if j in free else []
-            todo += [(i, j)] if i in free else []
-            for k, src in todo[0:most]:
-                pending[k].remove(src)
-                agg_pass(k, src)
-                if agg_done[k] == NP - 1:
-                    closed.append(k)
             dif_passes(n)
+            for k, src in ((j, i), (i, j)):
+                if k >= N_BURST:
+                    agg_pass(k, src)
+            if j == NP - 1 and i < N_BURST:
+                quarters.extend([(i, c) for c in range(4)])
+
+        def burst(most, tag):
+            for j, c in quarters[0:most]:
+                quarters.remove((j, c))
+                burst_quarter(j, c, tag)
+                if c == 3:
+                    to_finish.append(j)
 
         for n in range(n_units):
             transpose_unit(n)
-            leaving = closed
-            closed = []
-            ending = to_finish
-            to_finish = to_back
-            to_back = []
-            for j in freed:
-                free.add(j + 3)
-            freed = ending
+            ending = list(to_finish)
+            to_finish.clear()
             if n >= LAG:
-                multiply_unit(n - LAG, MAX_AGG)
+                multiply_unit(n - LAG)
                 square_unit(n - LAG)
-            for j in leaving:
-                evacuate(j, False)
-                to_back.append(j)
-            for j in to_back:
-                transpose_back(j, "A%d" % (j % 3))
+            burst(1 if n < 24 else 2, "X")
             for j in ending:
                 finish(j)
             if n == 0:
@@ -262,23 +268,25 @@ def tile_sheaflayer_kernel(tc, F, R, out_0, out_1):
             if n + 5 < NP:
                 load_f(n + 5)
 
-        for j in to_finish + to_back:
+        multiply_unit(last - 1)
+        square_unit(last - 1)
+        burst(2, "T0")
+        for j in to_finish:
             finish(j)
-        for j in freed + to_finish + to_back:
-            free.add(j + 3)
-        tail = []
-        for n in range(n_units - LAG, n_units):
-            multiply_unit(n, NP * NP)
-            for j in closed:
-                evacuate(j, j != 6)
-                tail.append(j)
-            closed = []
-            square_unit(n)
-        for j in tail:
-            transpose_back(j, "T%d" % (j - 4))
+        to_finish.clear()
+        for k, i in ((7, 6), (6, 7)):
+            agg_pass(k, i)
+        dif_passes(last)
+        for j in (7, 6):
+            evacuate(j, j == 6)
+        square_unit(last)
+        burst(2, "T0")
+        for j in (7, 6):
+            transpose_back(j, "T%d" % (j - 5))
+        for j in to_finish + [7, 6]:
             finish(j)
 
-        lt = psum.tile([P, n_units], F32, name="lt", tag="T0")
+        lt = psum.tile([P, n_units], F32, name="lt", tag="T3")
         nc.tensor.matmul(lt[:], lhsT=ones[:], rhs=acc[:], start=True, stop=True)
         nc.scalar.activation(
             out=junk[:, 0:n_units], in_=lt[:], func=ACT.Copy, scale=LOSS_WEIGHT, accum_out=tot[:, 0:1]

@@ -15,7 +15,7 @@ NP = 8
 D = 512
 B = 128
 P = 128
-LOSS_WEIGHT = 0.1 * 0.5 * 2.0
+LOSS_WEIGHT = 0.1 * 0.5 * 2.0 * 64.0
 
 FLOPS = 2 * NP * (NP - 1) * D * D * B
 BYTES = NP * (NP - 1) * D * D * 2 + NP * D * B * 2 + NP * D * B * 4 + 4
@@ -23,10 +23,17 @@ BYTES = NP * (NP - 1) * D * D * 2 + NP * D * B * 2 + NP * D * B * 4 + 4
 RAW_BUFS = 8
 SPLIT_BUFS = 4
 GROUPED_BUFS = 4
-STRIDED = [(n, s) for n in range(9) for s in range(2) if n < 4 or s == 1]
-VECTOR_BANKS = ((26, 1), (27, 1), (27, 3))
+STRIDED = [(n, s) for n in range(26) for s in range(2) if n < 4 or s == 1 and (n < 7 or n % 2 == 0)]
+VECTOR_BANKS = [(n, 3) for n in range(10, 28, 3)] + [(27, 1)]
+LATE = 99
+MAX_LATE = 3
 LAG = 2
-N_BURST = 6
+BANK = ("X", "A6", "A7", "X", "X", "T0", "A6", "A7")
+NEXT = {0: 3, 1: 6, 2: 7, 3: 4}
+LIVE = [0, 1, 2]
+EARLY = (0, 1, 2, 3)
+MAX_AGG = 2
+EV_S = False
 
 
 def tile_sheaflayer_kernel(tc, F, R, out_0, out_1):
@@ -90,13 +97,13 @@ def tile_sheaflayer_kernel(tc, F, R, out_0, out_1):
 
         def regroup_f(i):
             fg[i] = fpool.tile([P, D if i == 0 else 2 * D], BF16, name="fg", tag="fg", align_bytes=64)
-            nc.vector.tensor_copy(
+            nc.vector.tensor_scalar_mul(
                 out=fg[i][:, 0:D].rearrange("p (b t) -> p b t", t=4),
-                in_=fm[:, i, :].rearrange("p (t b) -> p b t", t=4),
+                in0=fm[:, i, :].rearrange("p (t b) -> p b t", t=4),
+                scalar1=0.125,
             )
 
         def negate_f(i):
-            nc.vector.tensor_scalar_mul(out=fm[:, i, :], in0=fm[:, i, :], scalar1=0.125)
             if i > 0:
                 nc.vector.tensor_scalar_mul(out=fg[i][:, D : 2 * D], in0=fg[i][:, 0:D], scalar1=-1.0)
 
@@ -147,41 +154,27 @@ def tile_sheaflayer_kernel(tc, F, R, out_0, out_1):
                 stop=stop,
             )
 
-        def dif_passes(n):
+        def dif_passes(n, tag="D"):
             i, j = units[n]
-            dif[n] = psum.tile([P, D], F32, name="dif", tag="D")
+            dif[n] = psum.tile([P, D], F32, name="dif%s" % tag, tag=tag)
             row_pass(dif[n], i, 0, n, 0, True, False)
             row_pass(dif[n], j, 1, n, 1, False, True)
 
         def agg_pass(j, i):
             if agg_done[j] == 0:
-                agg[j] = psum.tile([P, D], F32, name="agg%d" % j, tag="A%d" % j)
+                agg[j] = psum.tile([P, D], F32, name="agg%d" % j, tag=BANK[j])
             n, s = where(i, j)
             row_pass(agg[j], i, 0, n, s, agg_done[j] == 0, agg_done[j] == NP - 2)
             agg_done[j] += 1
-
-        def burst_quarter(j, c, tag):
-            if c == 0:
-                fin[j] = psum.tile([P, D], F32, name="fin%d" % j, tag=tag)
-            sources = [i for i in range(NP) if i != j]
-            for i in sources:
-                n, s = where(i, j)
-                at = D * s + P * c
-                nc.tensor.matmul_mx(
-                    out=fin[j][:, B * c : B * (c + 1)],
-                    lhsT=cd[n][:, at : at + P].bitcast(FP8X4),
-                    lhsT_scale=pl[n][:, at : at + P],
-                    rhs=fcd[i][:, 0:B].bitcast(FP8X4),
-                    rhs_scale=fpl[i][:, 0:B],
-                    start=i == sources[0],
-                    stop=i == sources[-1],
-                )
 
         def square_unit(n):
             nc.scalar.activation(out=junk[:], in_=dif[n][:], func=ACT.Square, accum_out=acc[:, n : n + 1])
 
         def evacuate(j, on_scalar):
-            aggT[j] = spool.tile([P, 2 * D], F32, name="split", tag="split")[:, 0:D]
+            if j in EARLY:
+                aggT[j] = opool.tile([P, D], F32, name="res", tag="res")
+            else:
+                aggT[j] = spool.tile([P, 2 * D], F32, name="split", tag="split")[:, 0:D]
             if on_scalar:
                 nc.scalar.copy(out=aggT[j][:], in_=agg[j][:])
             else:
@@ -195,7 +188,7 @@ def tile_sheaflayer_kernel(tc, F, R, out_0, out_1):
         def finish(j):
             res = aggT[j] if j in aggT else opool.tile([P, D], F32, name="res", tag="res")
             nc.vector.scalar_tensor_tensor(
-                out=res[:], in0=fin[j][:], scalar=0.125, in1=fm[:, j, :], op0=ALU.mult, op1=ALU.add
+                out=res[:], in0=fm[:, j, :], scalar=0.125, in1=fin[j][:], op0=ALU.mult, op1=ALU.add
             )
             nc.sync.dma_start(out=out_0[j].rearrange("(q t) b -> q (t b)", t=4), in_=res[:])
 
@@ -217,43 +210,40 @@ def tile_sheaflayer_kernel(tc, F, R, out_0, out_1):
             elif k % 2 == 1:
                 load_f(k // 2 + 1)
 
-        quarters = []
-        to_finish = []
+        pending = dict((j, []) for j in range(NP))
+        live = list(LIVE)
+        closed = []
+        to_back = []
 
-        def multiply_unit(n):
+        def note_unit(n):
             i, j = units[n]
-            dif_passes(n)
-            for k, src in ((j, i), (i, j)):
-                if k >= N_BURST:
-                    agg_pass(k, src)
-            if j == NP - 1 and i < N_BURST:
-                quarters.extend([(i, c) for c in range(4)])
+            pending[i].append(j)
+            pending[j].append(i)
 
-        def burst(most, tag):
-            for j, c in quarters[0:most]:
-                quarters.remove((j, c))
-                burst_quarter(j, c, tag)
-                if c == 3:
-                    to_finish.append(j)
+        def sum_passes(nodes, most):
+            todo = [(k, src) for k in nodes for src in pending[k]]
+            for k, src in todo[0:most]:
+                pending[k].remove(src)
+                agg_pass(k, src)
+                if agg_done[k] == NP - 1:
+                    closed.append(k)
+                    live.remove(k)
 
         for n in range(n_units):
             transpose_unit(n)
-            ending = list(to_finish)
-            to_finish.clear()
             if n >= LAG:
-                multiply_unit(n - LAG)
+                note_unit(n - LAG)
+                dif_passes(n - LAG)
+                sum_passes(list(live), MAX_AGG if n < LATE else MAX_LATE)
                 square_unit(n - LAG)
-            burst(1 if n < 24 else 2, "X")
-            for j in ending:
-                finish(j)
+            for j in to_back:
+                transpose_back(j, BANK[j])
+            new_f = [0, 1] if n == 0 else [n + 1] if n + 1 < NP else []
+            for i in new_f:
+                regroup_f(i)
             if n == 0:
-                regroup_f(0)
-                regroup_f(1)
                 split_block(1, 0)
                 split_block(1, 1)
-            elif n + 1 < NP:
-                regroup_f(n + 1)
-            new_f = [i for i in range(NP) if (i == 0 and n == 0) or i == n + 1]
             for s in range(2):
                 quantise_block(n, s)
                 if s == 0:
@@ -267,26 +257,45 @@ def tile_sheaflayer_kernel(tc, F, R, out_0, out_1):
                 load_more()
             if n + 5 < NP:
                 load_f(n + 5)
+            for j in to_back:
+                finish(j)
+                if j in NEXT:
+                    live.append(NEXT[j])
+            to_back.clear()
+            for j in closed:
+                evacuate(j, EV_S)
+                to_back.append(j)
+            closed.clear()
 
-        multiply_unit(last - 1)
+        note_unit(last - 1)
+        for j in range(4, 6):
+            if j not in live and agg_done[j] == 0:
+                live.append(j)
+        old = list(to_back)
+        sum_passes([k for k in live if k < 6], NP * NP)
+        for k in closed:
+            evacuate(k, k == 5)
+        dif_passes(last - 1)
         square_unit(last - 1)
-        burst(2, "T0")
-        for j in to_finish:
-            finish(j)
-        to_finish.clear()
-        for k, i in ((7, 6), (6, 7)):
-            agg_pass(k, i)
-        dif_passes(last)
-        for j in (7, 6):
-            evacuate(j, j == 6)
+        sum_passes([7, 6], NP * NP)
+        old.extend(closed)
+        for k in old[0:-1]:
+            transpose_back(k, BANK[k])
+            finish(k)
+        note_unit(last)
+        sum_passes([7, 6], NP * NP)
+        evacuate(7, True)
+        evacuate(6, False)
+        dif_passes(last, "T1")
         square_unit(last)
-        burst(2, "T0")
-        for j in (7, 6):
-            transpose_back(j, "T%d" % (j - 5))
-        for j in to_finish + [7, 6]:
-            finish(j)
+        for k in old[-1:]:
+            transpose_back(k, BANK[k])
+            finish(k)
+        for k in (7, 6):
+            transpose_back(k, "T%d" % (k - 4))
+            finish(k)
 
-        lt = psum.tile([P, n_units], F32, name="lt", tag="T3")
+        lt = psum.tile([P, n_units], F32, name="lt", tag="D")
         nc.tensor.matmul(lt[:], lhsT=ones[:], rhs=acc[:], start=True, stop=True)
         nc.scalar.activation(
             out=junk[:, 0:n_units], in_=lt[:], func=ACT.Copy, scale=LOSS_WEIGHT, accum_out=tot[:, 0:1]

@@ -23,15 +23,13 @@ BYTES = NP * (NP - 1) * D * D * 2 + NP * D * B * 2 + NP * D * B * 4 + 4
 RAW_BUFS = 8
 SPLIT_BUFS = 4
 GROUPED_BUFS = 4
-STRIDED = [(n, s) for n in range(26) for s in range(2) if n < 4 or s == 1 and (n < 7 or n % 2 == 0)]
-VECTOR_BANKS = [(n, 3) for n in range(10, 28, 3)] + [(27, 1)]
-LATE = 99
-MAX_LATE = 3
+STRIDED = [(n, s) for n in range(9) for s in range(2) if n < 4 or s == 1]
+VECTOR_BANKS = [(27, 1), (27, 3)]
 LAG = 2
-BANK = ("X", "A6", "A7", "X", "X", "T0", "A6", "A7")
-NEXT = {0: 3, 1: 6, 2: 7, 3: 4}
-LIVE = [0, 1, 2]
-EARLY = (0, 1, 2, 3)
+BANK = ("A0", "A1", "A2", "A3", "A0", "A3", "A1", "A2")
+NEXT = {0: 4, 1: 6, 2: 7, 3: 5}
+LIVE = [0, 1, 2, 3]
+EARLY = (0, 1, 2, 3, 4)
 MAX_AGG = 2
 EV_S = False
 
@@ -98,8 +96,8 @@ def tile_sheaflayer_kernel(tc, F, R, out_0, out_1):
         def regroup_f(i):
             fg[i] = fpool.tile([P, D if i == 0 else 2 * D], BF16, name="fg", tag="fg", align_bytes=64)
             nc.vector.tensor_scalar_mul(
-                out=fg[i][:, 0:D].rearrange("p (b t) -> p b t", t=4),
-                in0=fm[:, i, :].rearrange("p (t b) -> p b t", t=4),
+                out=fg[i][:, 0:D].rearrange("p (b c t) -> p b t c", c=4, t=4),
+                in0=fm[:, i, :].rearrange("p (t b c) -> p b t c", t=4, c=4),
                 scalar1=0.125,
             )
 
@@ -110,12 +108,18 @@ def tile_sheaflayer_kernel(tc, F, R, out_0, out_1):
         def quantise_f(i):
             nc.vector.quantize_mx(out=fcd[i][:].bitcast(FP8X4), scales=fpl[i][:], in_=fg[i][:])
 
+        slots = []
+
+        def next_slot():
+            slots.append(len(slots) % 4)
+            return "R%d" % slots[-1]
+
         def transpose_unit(n):
             for b in range(4):
                 s = b // 2
                 if b % 2 == 0:
                     grouped[n, s] = gpool.tile([P, 4 * D], BF16, name="grouped", tag="grouped", align_bytes=64)
-                tb = psum.tile([P, D], F32, name="tb%d" % b, tag="T%d" % b)
+                tb = psum.tile([P, D], F32, name="tb%d" % b, tag=next_slot())
                 for x in range(4):
                     if (n, s) in STRIDED:
                         consumed.add((n, s))
@@ -154,9 +158,9 @@ def tile_sheaflayer_kernel(tc, F, R, out_0, out_1):
                 stop=stop,
             )
 
-        def dif_passes(n, tag="D"):
+        def dif_passes(n):
             i, j = units[n]
-            dif[n] = psum.tile([P, D], F32, name="dif%s" % tag, tag=tag)
+            dif[n] = psum.tile([P, D], F32, name="dif", tag=next_slot())
             row_pass(dif[n], i, 0, n, 0, True, False)
             row_pass(dif[n], j, 1, n, 1, False, True)
 
@@ -234,7 +238,7 @@ def tile_sheaflayer_kernel(tc, F, R, out_0, out_1):
             if n >= LAG:
                 note_unit(n - LAG)
                 dif_passes(n - LAG)
-                sum_passes(list(live), MAX_AGG if n < LATE else MAX_LATE)
+                sum_passes(list(live), MAX_AGG)
                 square_unit(n - LAG)
             for j in to_back:
                 transpose_back(j, BANK[j])
@@ -268,17 +272,15 @@ def tile_sheaflayer_kernel(tc, F, R, out_0, out_1):
             closed.clear()
 
         note_unit(last - 1)
-        for j in range(4, 6):
-            if j not in live and agg_done[j] == 0:
-                live.append(j)
         old = list(to_back)
         sum_passes([k for k in live if k < 6], NP * NP)
+        old.extend(closed)
         for k in closed:
-            evacuate(k, k == 5)
+            evacuate(k, True)
+        closed.clear()
         dif_passes(last - 1)
         square_unit(last - 1)
         sum_passes([7, 6], NP * NP)
-        old.extend(closed)
         for k in old[0:-1]:
             transpose_back(k, BANK[k])
             finish(k)
@@ -286,16 +288,13 @@ def tile_sheaflayer_kernel(tc, F, R, out_0, out_1):
         sum_passes([7, 6], NP * NP)
         evacuate(7, True)
         evacuate(6, False)
-        dif_passes(last, "T1")
+        dif_passes(last)
         square_unit(last)
-        for k in old[-1:]:
+        for k in old[-1:] + [7, 6]:
             transpose_back(k, BANK[k])
             finish(k)
-        for k in (7, 6):
-            transpose_back(k, "T%d" % (k - 4))
-            finish(k)
 
-        lt = psum.tile([P, n_units], F32, name="lt", tag="D")
+        lt = psum.tile([P, n_units], F32, name="lt", tag=next_slot())
         nc.tensor.matmul(lt[:], lhsT=ones[:], rhs=acc[:], start=True, stop=True)
         nc.scalar.activation(
             out=junk[:, 0:n_units], in_=lt[:], func=ACT.Copy, scale=LOSS_WEIGHT, accum_out=tot[:, 0:1]

from contextlib import ExitStack

import concourse.mybir as mybir
from concourse.masks import make_identity

F32 = mybir.dt.float32
BF16 = mybir.dt.bfloat16
U32 = mybir.dt.uint32
U8 = mybir.dt.uint8
FP8X4 = mybir.dt.float8_e4m3fn_x4
ALU = mybir.AluOpType
ACT = mybir.ActivationFunctionType

NP = 8
D = 512
B = 128
P = 128
LOSS_WEIGHT = 0.1 * 0.5 * 2.0 * 64.0

FLOPS = 2 * NP * (NP - 1) * D * D * B
BYTES = NP * (NP - 1) * D * D * 2 + NP * D * B * 2 + NP * D * B * 4 + 4

RAW_BUFS = 8
SPLIT_BUFS = 4
GROUPED_BUFS = 4
STRIDED = [(n, s) for n in range(9) for s in range(2) if n < 4 or s == 1]
VECTOR_BANKS = [(27, 1), (27, 3)]
LAG = 2
BANK = ("A0", "A1", "A2", "A3", "A0", "A3", "A1", "A2")
NEXT = {0: 4, 1: 6, 2: 7, 3: 5}
LIVE = [0, 1, 2, 3]
EARLY = (0, 1, 2, 3, 4)
MAX_AGG = 2
EV_S = False


def tile_sheaflayer_kernel(tc, F, R, out_0, out_1):
    nc = tc.nc
    units = [(i, j) for i in range(NP) for j in range(i + 1, NP)]
    n_units = len(units)
    last = n_units - 1
    unit_of = dict((pair, n) for n, pair in enumerate(units))

    def where(i, j):
        return (unit_of[(i, j)], 0) if i < j else (unit_of[(j, i)], 1)

    with ExitStack() as ctx:
        ctx.enter_context(tc.manual_schedule())
        keep = ctx.enter_context(tc.tile_pool(name="keep", bufs=1))
        rawpool = ctx.enter_context(tc.tile_pool(name="rawpool", bufs=RAW_BUFS))
        spool = ctx.enter_context(tc.tile_pool(name="spool", bufs=SPLIT_BUFS))
        gpool = ctx.enter_context(tc.tile_pool(name="gpool", bufs=GROUPED_BUFS))
        fpool = ctx.enter_context(tc.tile_pool(name="fpool", bufs=2))
        opool = ctx.enter_context(tc.tile_pool(name="opool", bufs=3))
        psum = ctx.enter_context(tc.psum_pool(name="psum", bufs=1))

        ident = keep.tile([P, P], F32, name="ident")
        make_identity(nc, ident[:])
        ones = keep.tile([P, P], F32, name="ones")
        nc.vector.memset(ones[:], 1.0)
        acc = keep.tile([P, n_units], F32, name="acc")
        tot = keep.tile([P, 1], F32, name="tot")
        junk = keep.tile([P, D], F32, name="junk")
        fm = keep.tile([P, NP, D], BF16, name="fm")
        fcd = [keep.tile([P, B if i == 0 else 2 * B], U32, name="fcd%d" % i, align_bytes=64) for i in range(NP)]
        fpl = [keep.tile([P, B if i == 0 else 2 * B], U8, name="fpl%d" % i, align_bytes=64) for i in range(NP)]
        cd = [keep.tile([P, 2 * D], U32, name="cd%d" % n, align_bytes=64) for n in range(n_units)]
        pl = [keep.tile([P, 2 * D], U8, name="pl%d" % n, align_bytes=64) for n in range(n_units)]
        raw = {}
        fg = {}
        split = {}
        grouped = {}
        dif = {}
        agg = {}
        agg_done = dict((j, 0) for j in range(NP))
        aggT = {}
        fin = {}

        def load_f(i):
            nc.sync.dma_start(out=fm[:, i, :], in_=F[i].rearrange("(q t) b -> q (t b)", t=4))

        def load_block(n, s):
            i, j = units[n] if s == 0 else units[n][::-1]
            raw[n, s] = rawpool.tile([P, 4 * D], BF16, name="raw", tag="raw")
            nc.sync.dma_start(out=raw[n, s][:], in_=R[i, j].rearrange("(p c) e -> p (c e)", c=4))

        def split_block(n, s):
            if (n, s) not in STRIDED:
                consumed.add((n, s))
                split[n, s] = spool.tile([P, 2 * D], F32, name="split", tag="split")
                nc.vector.tensor_copy(
                    out=split[n, s][:].rearrange("p (c u q) -> p c q u", c=4, u=2),
                    in_=raw[n, s][:].bitcast(F32).rearrange("p (c q u) -> p c q u", c=4, u=2),
                )

        def regroup_f(i):
            fg[i] = fpool.tile([P, D if i == 0 else 2 * D], BF16, name="fg", tag="fg", align_bytes=64)
            nc.vector.tensor_scalar_mul(
                out=fg[i][:, 0:D].rearrange("p (b c t) -> p b t c", c=4, t=4),
                in0=fm[:, i, :].rearrange("p (t b c) -> p b t c", t=4, c=4),
                scalar1=0.125,
            )

        def negate_f(i):
            if i > 0:
                nc.vector.tensor_scalar_mul(out=fg[i][:, D : 2 * D], in0=fg[i][:, 0:D], scalar1=-1.0)

        def quantise_f(i):
            nc.vector.quantize_mx(out=fcd[i][:].bitcast(FP8X4), scales=fpl[i][:], in_=fg[i][:])

        slots = []

        def next_slot():
            slots.append(len(slots) % 4)
            return "R%d" % slots[-1]

        def transpose_unit(n):
            for b in range(4):
                s = b // 2
                if b % 2 == 0:
                    grouped[n, s] = gpool.tile([P, 4 * D], BF16, name="grouped", tag="grouped", align_bytes=64)
                tb = psum.tile([P, D], F32, name="tb%d" % b, tag=next_slot())
                for x in range(4):
                    if (n, s) in STRIDED:
                        consumed.add((n, s))
                        col = D * (b % 2) + 2 * P * (x // 2) + x % 2
                        src = raw[n, s][:].bitcast(F32)[:, col : col + 2 * P - 1 : 2]
                    else:
                        col = D * (b % 2) + P * x
                        src = split[n, s][:, col : col + P]
                    nc.tensor.transpose(tb[:, P * x : P * (x + 1)], src, ident[:])
                dst = (
                    grouped[n, s][:]
                    .bitcast(F32)[:, D * (b % 2) : D * (b % 2 + 1)]
                    .rearrange("p (c d u) -> p c d u", c=2, u=2)
                )
                src = tb[:].rearrange("p (c u d) -> p c d u", c=2, u=2)
                if (n, b) in VECTOR_BANKS:
                    nc.vector.tensor_copy(out=dst, in_=src)
                else:
                    nc.scalar.copy(out=dst, in_=src)

        def quantise_block(n, s):
            nc.vector.quantize_mx(
                out=cd[n][:, D * s : D * (s + 1)].bitcast(FP8X4),
                scales=pl[n][:, D * s : D * (s + 1)],
                in_=grouped[n, s][:],
            )

        def row_pass(bank, i_src, sign, n, s, start, stop):
            nc.tensor.matmul_mx(
                out=bank[:],
                lhsT=fcd[i_src][:, B * sign : B * (sign + 1)].bitcast(FP8X4),
                lhsT_scale=fpl[i_src][:, B * sign : B * (sign + 1)],
                rhs=cd[n][:, D * s : D * (s + 1)].bitcast(FP8X4),
                rhs_scale=pl[n][:, D * s : D * (s + 1)],
                start=start,
                stop=stop,
            )

        def dif_passes(n):
            i, j = units[n]
            dif[n] = psum.tile([P, D], F32, name="dif", tag=next_slot())
            row_pass(dif[n], i, 0, n, 0, True, False)
            row_pass(dif[n], j, 1, n, 1, False, True)

        def agg_pass(j, i):
            if agg_done[j] == 0:
                agg[j] = psum.tile([P, D], F32, name="agg%d" % j, tag=BANK[j])
            n, s = where(i, j)
            row_pass(agg[j], i, 0, n, s, agg_done[j] == 0, agg_done[j] == NP - 2)
            agg_done[j] += 1

        def square_unit(n):
            nc.scalar.activation(out=junk[:], in_=dif[n][:], func=ACT.Square, accum_out=acc[:, n : n + 1])

        def evacuate(j, on_scalar):
            if j in EARLY:
                aggT[j] = opool.tile([P, D], F32, name="res", tag="res")
            else:
                aggT[j] = spool.tile([P, 2 * D], F32, name="split", tag="split")[:, 0:D]
            if on_scalar:
                nc.scalar.copy(out=aggT[j][:], in_=agg[j][:])
            else:
                nc.vector.tensor_copy(out=aggT[j][:], in_=agg[j][:])

        def transpose_back(j, tag):
            fin[j] = psum.tile([P, D], F32, name="fin%d" % j, tag=tag)
            for t in range(4):
                nc.tensor.transpose(fin[j][:, P * t : P * (t + 1)], aggT[j][:, P * t : P * (t + 1)], ident[:])

        def finish(j):
            res = aggT[j] if j in aggT else opool.tile([P, D], F32, name="res", tag="res")
            nc.vector.scalar_tensor_tensor(
                out=res[:], in0=fm[:, j, :], scalar=0.125, in1=fin[j][:], op0=ALU.mult, op1=ALU.add
            )
            nc.sync.dma_start(out=out_0[j].rearrange("(q t) b -> q (t b)", t=4), in_=res[:])

        blocks = [(n, s) for n in range(n_units) for s in range(2)]

        consumed = set()

        def load_more():
            k = len(raw)
            while k < len(blocks) and (k < RAW_BUFS or blocks[k - RAW_BUFS] in consumed):
                load_block(*blocks[k])
                k += 1

        for k in range(RAW_BUFS):
            load_block(*blocks[k])
            if k == 1:
                load_f(0)
                load_f(1)
            elif k % 2 == 1:
                load_f(k // 2 + 1)

        pending = dict((j, []) for j in range(NP))
        live = list(LIVE)
        closed = []
        to_back = []

        def note_unit(n):
            i, j = units[n]
            pending[i].append(j)
            pending[j].append(i)

        def sum_passes(nodes, most):
            todo = [(k, src) for k in nodes for src in pending[k]]
            for k, src in todo[0:most]:
                pending[k].remove(src)
                agg_pass(k, src)
                if agg_done[k] == NP - 1:
                    closed.append(k)
                    live.remove(k)

        for n in range(n_units):
            transpose_unit(n)
            if n >= LAG:
                note_unit(n - LAG)
                dif_passes(n - LAG)
                sum_passes(list(live), MAX_AGG)
                square_unit(n - LAG)
            for j in to_back:
                transpose_back(j, BANK[j])
            new_f = [0, 1] if n == 0 else [n + 1] if n + 1 < NP else []
            for i in new_f:
                regroup_f(i)
            if n == 0:
                split_block(1, 0)
                split_block(1, 1)
            for s in range(2):
                quantise_block(n, s)
                if s == 0:
                    for i in new_f:
                        negate_f(i)
                else:
                    for i in new_f:
                        quantise_f(i)
                if n + 2 < n_units:
                    split_block(n + 2, s)
                load_more()
            if n + 5 < NP:
                load_f(n + 5)
            for j in to_back:
                finish(j)
                if j in NEXT:
                    live.append(NEXT[j])
            to_back.clear()
            for j in closed:
                evacuate(j, EV_S)
                to_back.append(j)
            closed.clear()

        note_unit(last - 1)
        old = list(to_back)
        sum_passes([k for k in live if k < 6], NP * NP)
        old.extend(closed)
        for k in closed:
            evacuate(k, True)
        closed.clear()
        dif_passes(last - 1)
        square_unit(last - 1)
        sum_passes([7, 6], NP * NP)
        for k in old[0:-1]:
            transpose_back(k, BANK[k])
            finish(k)
        note_unit(last)
        sum_passes([7, 6], NP * NP)
        evacuate(7, True)
        evacuate(6, False)
        dif_passes(last)
        square_unit(last)
        for k in old[-1:] + [7, 6]:
            transpose_back(k, BANK[k])
            finish(k)

        lt = psum.tile([P, n_units], F32, name="lt", tag=next_slot())
        nc.tensor.matmul(lt[:], lhsT=ones[:], rhs=acc[:], start=True, stop=True)
        nc.scalar.activation(
            out=junk[:, 0:n_units], in_=lt[:], func=ACT.Copy, scale=LOSS_WEIGHT, accum_out=tot[:, 0:1]
        )
        loss_view = out_1
        for k in range(2 - len(out_1.shape)):
            loss_view = loss_view.unsqueeze(0)
        nc.sync.dma_start(out=loss_view, in_=tot[0:1, 0:1])
